import numpy as np
import ml_dtypes


def mxq(x, axis, fmt="e4m3"):
    dtype, down = {"e4m3": (ml_dtypes.float8_e4m3fn, 7), "e5m2": (ml_dtypes.float8_e5m2, 14)}[fmt]
    v = np.moveaxis(np.asarray(x, np.float32).astype(ml_dtypes.bfloat16).astype(np.float64), axis, -1)
    blocks = v.reshape(v.shape[:-1] + (-1, 32))
    amax = np.abs(blocks).max(-1, keepdims=True)
    byte = np.maximum(np.where(amax > 0, np.frexp(amax)[1] - 1 + 127, 0) - down, 1)
    scale = np.exp2(byte - 127.0)
    codes = (blocks / scale).astype(np.float32).astype(dtype).astype(np.float64)
    return np.moveaxis((codes * scale).reshape(v.shape), -1, axis)


WIDE = False


def mx_kscale(k):
    if not WIDE:
        return np.ones(k)
    levels = np.array([10, -10, 5, -5, 0])
    if k % 512:
        return np.exp2(np.random.permutation(np.resize(levels, k // 32))).repeat(32)
    a = np.empty((k // 512, 16))
    for p in range(k // 512):
        a[p, :8] = np.random.permutation(np.resize(levels, 8))
        for g in range(8):
            far = levels[np.abs(levels - a[p, g]) >= 10]
            a[p, g + 8] = far[np.random.randint(len(far))]
    return np.exp2(a.ravel()).repeat(32)


BF16 = ml_dtypes.bfloat16


def bf(x):
    return np.asarray(x, np.float32).astype(BF16)


def f64(x):
    return np.asarray(x).astype(np.float64)


B, CI, CO, N, KM, M = 2, 128, 128, 1024, 32, 512
R = 6.0
A = np.sqrt(R) / N ** 0.25


def draw0():
    u = mx_kscale(CI * KM)[::KM]
    t = mx_kscale(M)
    return {
        "x": bf((np.random.standard_normal((B, CI, N)) + A) * u[None, :, None]),
        "wbases": bf((np.random.standard_normal((B, N, M)) + A) / (R * np.sqrt(N))),
        "bases": bf(np.random.standard_normal((B, N, M)) / np.sqrt(M) / t),
        "weights": bf(np.random.standard_normal((CI, CO, KM)) / np.sqrt(CI * KM) / u[:, None, None]),
        "D": bf(np.random.standard_normal((KM, M)) * t),
    }


def core(x, wbases, bases, weights, D):
    x_hat = f64(x) @ f64(wbases)[:, :, :M]
    z = (x_hat[:, :, None, :] * f64(D)[None, None, :, :]).reshape(B, CI * KM, M)
    w2 = f64(weights).transpose(0, 2, 1).reshape(CI * KM, CO)
    y_hat = mxq(w2, 0, "e4m3").T @ mxq(z, 1, "e4m3")
    return mxq(y_hat, 2, "e4m3") @ mxq(f64(bases)[:, :, :M], 2, "e4m3").transpose(0, 2, 1)


def e4m3fn_bytes(y):
    return np.clip(np.asarray(y, np.float64), -448.0, 448.0).astype(np.float32).astype(ml_dtypes.float8_e4m3fn).view(np.uint8)


def e4m3fn_values(b):
    return np.asarray(b, np.uint8).view(ml_dtypes.float8_e4m3fn).astype(np.float64)


def setup_inputs():
    d = draw0()
    x0 = np.asarray(d['bases']).astype(np.float64)
    s = (np.max(np.abs(x0), axis=(0, 1), keepdims=True) / 448.0).astype(np.float32)
    out = {}
    for k, v in d.items():
        if k == 'bases':
            out['bases_bytes'] = e4m3fn_bytes(x0 / s.astype(np.float64))
            out['bases_scale'] = s
        else:
            out[k] = v
    return out


def reference(x, wbases, bases_bytes, bases_scale, weights, D):
    return core(x, wbases, e4m3fn_values(bases_bytes) * bases_scale.astype(np.float64), weights, D)

@@ -1,0 +1,372 @@
+from contextlib import ExitStack
+
+import concourse.mybir as mybir
+from concourse.masks import make_identity
+
+FLOPS = 1610612736
+
+F32 = mybir.dt.float32
+BF16 = mybir.dt.bfloat16
+U32 = mybir.dt.uint32
+U8 = mybir.dt.uint8
+FP8 = mybir.dt.float8_e4m3fn
+FP8X4 = mybir.dt.float8_e4m3fn_x4
+MULT = mybir.AluOpType.mult
+COPY = mybir.ActivationFunctionType.Copy
+
+P = 128
+NB = (2, 3, 2, 3, 3, 3, 3, 3)
+
+
+def tile_phydgalerkinconv_kernel(tc, x, wbases, bases_bytes, bases_scale, weights, D, out):
+    nc = tc.nc
+    with ExitStack() as ctx:
+        keep = ctx.enter_context(tc.tile_pool(name="keep", bufs=1))
+        work = ctx.enter_context(tc.tile_pool(name="work", bufs=2))
+        psum = ctx.enter_context(tc.psum_pool(name="psum", bufs=1))
+
+        sc4 = keep.tile([P, 4], F32, name="sc4")
+        nc.sync.dma_start(out=sc4[:], in_=bases_scale.rearrange("a b (p c) -> p (a b c)", c=4))
+        dpad = keep.tile([P, 512], BF16, name="dpad")
+        nc.vector.memset(dpad[:], 0.0)
+        nc.sync.dma_start(out=dpad[0:32, :], in_=D)
+        bytes_sb = [keep.tile([P, 2, 4, 512], U8, name="bytes0"), keep.tile([P, 2, 4, 512], U8, name="bytes1")]
+        x_sb = [keep.tile([P, 1024], BF16, name="x0"), keep.tile([P, 1024], BF16, name="x1")]
+        wb_sb = [keep.tile([P, 8, 512], BF16, name="wb0"), keep.tile([P, 8, 512], BF16, name="wb1")]
+        w_raw = keep.tile([P, P, 32], BF16, name="w_raw")
+
+        def load_bytes(b, h):
+            nc.sync.dma_start(
+                out=bytes_sb[b][:, h], in_=bases_bytes[b].rearrange("(h p c) k -> h p c k", h=2, c=4)[h]
+            )
+
+        def load_wb(b):
+            for q in range(2):
+                nc.sync.dma_start(
+                    out=wb_sb[b][:, 4 * q : 4 * q + 4, :],
+                    in_=wbases[b].rearrange("(c p) k -> p c k", p=P)[:, 4 * q : 4 * q + 4, :],
+                )
+
+        load_bytes(0, 0)
+        nc.sync.dma_start(out=x_sb[0][:], in_=x[0])
+        load_bytes(0, 1)
+        load_wb(0)
+        load_bytes(1, 0)
+        load_bytes(1, 1)
+        for q in range(2):
+            nc.sync.dma_start(
+                out=w_raw[:, 64 * q : 64 * q + 64, :],
+                in_=weights.rearrange("i o j -> o i j")[:, 64 * q : 64 * q + 64, :],
+            )
+        nc.sync.dma_start(out=x_sb[1][:], in_=x[1])
+        load_wb(1)
+
+        ident_f = keep.tile([P, P], F32, name="ident_f")
+        make_identity(nc, ident_f[:])
+        ident_b = keep.tile([P, P], BF16, name="ident_b")
+        sel = keep.tile([P, 4, P], BF16, name="sel")
+        scale_rep = keep.tile([P, 512], F32, name="scale_rep")
+        drep = keep.tile([P, 4, P, 4], BF16, name="drep")
+        dt = keep.tile([P, 4, 32], BF16, name="dt")
+        xt = [keep.tile([P, 8, P], BF16, name="xt0"), keep.tile([P, 8, P], BF16, name="xt1")]
+        bc = [keep.tile([P, 1024], U32, name="bc0", align_bytes=64), keep.tile([P, 1024], U32, name="bc1", align_bytes=64)]
+        bs = [keep.tile([P, 1024], U8, name="bs0", align_bytes=64), keep.tile([P, 1024], U8, name="bs1", align_bytes=64)]
+        wg = keep.tile([P, 4096], BF16, name="wg", align_bytes=64)
+        wc = keep.tile([P, 8, P], U32, name="wc", align_bytes=64)
+        ws = keep.tile([P, 8, P], U8, name="ws", align_bytes=64)
+        warm = keep.tile([P, 1], F32, name="warm")
+
+        ctx.enter_context(tc.manual_schedule())
+
+        nc.vector.memset(warm[:], 0.0)
+        nc.scalar.activation(out=warm[:], in_=warm[:], func=COPY, scale=1.0)
+        nc.vector.tensor_copy(out=ident_b[:], in_=ident_f[:])
+        for t in range(4):
+            nc.vector.tensor_copy(
+                out=sel[:, t, :].rearrange("p (i q) -> p i q", q=8),
+                in_=ident_b[:, t:32:4].unsqueeze(1).to_broadcast([P, 16, 8]),
+            )
+
+        sc_ps = psum.tile([P, 4, P], F32, name="sc_ps", tag="A", bufs=3)
+        for c in range(4):
+            nc.tensor.transpose(sc_ps[:, c, :], sc4[:, c : c + 1].to_broadcast([P, P]), ident_f[:])
+        nc.vector.tensor_copy(
+            out=scale_rep[:].rearrange("p (n c) -> p n c", c=4), in_=sc_ps[:].rearrange("p c n -> p n c")
+        )
+
+        dt_ps = psum.tile([P, 4, P], BF16, name="dt_ps", tag="W", bufs=2)
+        for t in range(4):
+            nc.tensor.transpose(dt_ps[:, t, :], dpad[:, t::4], ident_b[:])
+        nc.scalar.copy(out=dt[:], in_=dt_ps[:, :, 0:32])
+        d_perm = dpad[:].rearrange("p (m t) -> p t m", t=4)
+        for h in range(2):
+            d_ps = psum.tile([P, 4, 2, P], BF16, name="d_ps", tag="A", bufs=3)
+            for tj in range(4):
+                nc.tensor.matmul(
+                    d_ps[:, tj], lhsT=sel[:, tj, :], rhs=d_perm[:, 2 * h : 2 * h + 2, :], start=True, stop=True
+                )
+            (nc.vector.tensor_copy if h == 0 else nc.scalar.copy)(
+                out=drep[:, 2 * h : 2 * h + 2], in_=d_ps[:].rearrange("p j t m -> p t m j")
+            )
+
+        bb = {}
+        bg = {}
+
+        def bases_scale_rows(b, h):
+            bb[b, h] = work.tile([P, 4, 512], BF16, name="bb")
+            for c in range(4):
+                nc.vector.tensor_tensor(
+                    out=bb[b, h][:, c, :], in0=bytes_sb[b][:, h, c, :].bitcast(FP8), in1=scale_rep[:], op=MULT
+                )
+
+        def bases_turn(b, h):
+            words = bb[b, h][:].rearrange("p c k -> p (c k)").bitcast(F32)
+            bg[b, h] = work.tile([P, 2048], BF16, name="bg", align_bytes=64)
+            dst = bg[b, h][:].bitcast(F32).rearrange("p (c n u) -> p c n u", c=4, u=2)
+            for c2 in range(2):
+                ps = psum.tile([P, 2, 2, P], F32, name="b_ps", tag="W", bufs=2)
+                for cc in range(2):
+                    c = 2 * c2 + cc
+                    for u in range(2):
+                        nc.tensor.transpose(ps[:, cc, u, :], words[:, 256 * c + u : 256 * (c + 1) : 2], ident_f[:])
+                nc.scalar.copy(out=dst[:, 2 * c2 : 2 * c2 + 2], in_=ps[:].rearrange("p c u n -> p c n u"))
+
+        def bases_quant(b, h):
+            cols = slice(512 * h, 512 * h + 512)
+            nc.vector.quantize_mx(out=bc[b][:, cols].bitcast(FP8X4), scales=bs[b][:, cols], in_=bg[b, h][:])
+
+        def x_turn(b):
+            ps = psum.tile([P, 8, P], BF16, name="x_ps", tag="W", bufs=2)
+            for c in range(8):
+                nc.tensor.transpose(ps[:, c, :], x_sb[b][:, P * c : P * (c + 1)], ident_b[:])
+            nc.scalar.copy(out=xt[b][:], in_=ps[:])
+
+        xh = {}
+        rep = {}
+        xsc = {}
+        xr = {}
+        zb = {}
+        wt = {}
+        z = {}
+        zc = {}
+        zs = {}
+        y_ps = {}
+
+        def step1(u):
+            b, t = divmod(u, 4)
+            xh[u] = psum.tile([P, P], F32, name="xh", tag="X", bufs=2)
+            for c in range(8):
+                nc.tensor.matmul(
+                    xh[u][:], lhsT=wb_sb[b][:, c, t::4], rhs=xt[b][:, c, :], start=(c == 0), stop=(c == 7)
+                )
+
+        def spread(u):
+            na = 16 * (8 - NB[u])
+            rep[u] = work.tile([P, P, 8], F32, name="rep")
+            nc.scalar.copy(
+                out=rep[u][:, :na, :], in_=xh[u][:, :na].unsqueeze(2).to_broadcast([P, na, 8])
+            )
+            xsc[u] = work.tile([P, 64], F32, name="xsc")
+            nc.scalar.copy(out=xsc[u][:, : P - na], in_=xh[u][:, na:])
+
+        def turn_a(u, part):
+            lo, hi = (0, 4) if part == 0 else (4, 8 - NB[u])
+            if hi == lo:
+                return
+            xr[u, part] = psum.tile([P, hi - lo, P], F32, name="xr", tag="A", bufs=3)
+            flat = rep[u][:].rearrange("p i r -> p (i r)")
+            for g in range(lo, hi):
+                nc.tensor.transpose(xr[u, part][:, g - lo, :], flat[:, P * g : P * (g + 1)], ident_f[:])
+
+        def product_a(u, part):
+            t = u % 4
+            lo, hi = (0, 4) if part == 0 else (4, 8 - NB[u])
+            if part == 0:
+                z[u] = work.tile([P, 8, P, 4], BF16, name="z", bufs=3, align_bytes=64)
+            if hi == lo:
+                return
+            shape = [P, hi - lo, P, 4]
+            nc.vector.tensor_tensor(
+                out=z[u][:, lo:hi],
+                in0=xr[u, part][:].unsqueeze(3).to_broadcast(shape),
+                in1=drep[:, t].unsqueeze(1).to_broadcast(shape),
+                op=MULT,
+            )
+
+        def product_b(u):
+            t = u % 4
+            zb[u] = work.tile([P, 4 * 512], BF16, name="zb")
+            for i in range(16 * NB[u]):
+                nc.scalar.activation(
+                    out=zb[u][:, 32 * i : 32 * i + 32], in_=dt[:, t, :], func=COPY, scale=xsc[u][:, i : i + 1]
+                )
+
+        def turn_b(u):
+            words = zb[u][:].bitcast(F32)
+            for g0 in range(0, NB[u], 2):
+                n = min(2, NB[u] - g0)
+                wt[u, g0] = psum.tile([P, n, 2, P], F32, name="wt", tag="W", bufs=2)
+                for g in range(n):
+                    base = 256 * (g0 + g)
+                    for w in range(2):
+                        nc.tensor.transpose(wt[u, g0][:, g, w, :], words[:, base + w : base + 256 : 2], ident_f[:])
+
+        def gather_b(u):
+            na = 8 - NB[u]
+            dst = z[u][:].rearrange("p g k t -> p (g k t)").bitcast(F32).rearrange("p (g k w) -> p g k w", g=8, w=2)
+            for g0 in range(0, NB[u], 2):
+                n = min(2, NB[u] - g0)
+                nc.scalar.copy(
+                    out=dst[:, na + g0 : na + g0 + n], in_=wt[u, g0][:].rearrange("p g w k -> p g k w")
+                )
+
+        def quant(u, half):
+            if half == 0:
+                zc[u] = work.tile([P, 8, P], U32, name="zc", bufs=8, align_bytes=64)
+                zs[u] = work.tile([P, 8, P], U8, name="zs", bufs=8, align_bytes=64)
+            gs = slice(4 * half, 4 * half + 4)
+            nc.vector.quantize_mx(
+                out=zc[u][:, gs, :].rearrange("p g k -> p (g k)").bitcast(FP8X4),
+                scales=zs[u][:, gs, :].rearrange("p g k -> p (g k)"),
+                in_=z[u][:, gs].rearrange("p g k t -> p (g k t)"),
+            )
+
+        def multiply(u):
+            b, t = divmod(u, 4)
+            if t == 0:
+                y_ps[b] = psum.tile([P, 4, P], F32, name="y_ps", tag="Y", bufs=1)
+            for g in range(8):
+                nc.tensor.matmul_mx(
+                    out=y_ps[b][:, t, :],
+                    lhsT=zc[u][:, g, :].bitcast(FP8X4),
+                    lhsT_scale=zs[u][:, g, :],
+                    rhs=wc[:, g, :].bitcast(FP8X4),
+                    rhs_scale=ws[:, g, :],
+                    start=(g == 0),
+                    stop=(g == 7),
+                )
+
+        def weights_turn(g2):
+            words = w_raw[:].rearrange("p i j -> p (i j)").bitcast(F32)
+            dst = wg[:].bitcast(F32).rearrange("p (g n w) -> p g n w", g=8, w=2)
+            ps = psum.tile([P, 2, 2, P], F32, name="w_ps", tag="W", bufs=2)
+            for g in range(2):
+                base = 256 * (2 * g2 + g)
+                for w in range(2):
+                    nc.tensor.transpose(ps[:, g, w, :], words[:, base + w : base + 256 : 2], ident_f[:])
+            nc.scalar.copy(out=dst[:, 2 * g2 : 2 * g2 + 2], in_=ps[:].rearrange("p g w n -> p g n w"))
+
+        def weights_quant(half):
+            gs = slice(4 * half, 4 * half + 4)
+            nc.vector.quantize_mx(
+                out=wc[:, gs, :].rearrange("p g n -> p (g n)").bitcast(FP8X4),
+                scales=ws[:, gs, :].rearrange("p g n -> p (g n)"),
+                in_=wg[:, 2048 * half : 2048 * half + 2048],
+            )
+
+        yc = {}
+        ys = {}
+        yb = {}
+        o_ps = {}
+        o_sb = {}
+
+        def y_out(b):
+            yb[b] = work.tile([P, P, 4], BF16, name="yb", align_bytes=64)
+            nc.scalar.copy(out=yb[b][:], in_=y_ps[b][:].rearrange("p t o -> p o t"))
+
+        def y_quant(b):
+            yc[b] = work.tile([P, P], U32, name="yc", align_bytes=64)
+            ys[b] = work.tile([P, P], U8, name="ys", align_bytes=64)
+            nc.vector.quantize_mx(
+                out=yc[b][:].bitcast(FP8X4), scales=ys[b][:], in_=yb[b][:].rearrange("p o t -> p (o t)")
+            )
+
+        def step3(b):
+            for h in range(2):
+                o_ps[b, h] = psum.tile([P, 512], F32, name="o_ps", tag="W", bufs=2)
+                cols = slice(512 * h, 512 * h + 512)
+                nc.tensor.matmul_mx(
+                    out=o_ps[b, h][:],
+                    lhsT=yc[b][:].bitcast(FP8X4),
+                    lhsT_scale=ys[b][:],
+                    rhs=bc[b][:, cols].bitcast(FP8X4),
+                    rhs_scale=bs[b][:, cols],
+                    start=True,
+                    stop=True,
+                )
+
+        def store(b, h):
+            o_sb[b, h] = work.tile([P, 512], F32, name="o_sb")
+            (nc.vector.tensor_copy if b == 1 and h == 0 else nc.scalar.copy)(
+                out=o_sb[b, h][:].rearrange("o (p c) -> o p c", c=4),
+                in_=o_ps[b, h][:].rearrange("o (c p) -> o p c", c=4),
+            )
+            nc.sync.dma_start(out=out[b][:, 512 * h : 512 * h + 512], in_=o_sb[b, h][:])
+
+        bases_scale_rows(0, 0)
+        bases_turn(0, 0)
+        x_turn(0)
+        bases_scale_rows(0, 1)
+        bases_turn(0, 1)
+        bases_quant(0, 0)
+        step1(0)
+        spread(0)
+        step1(1)
+        turn_a(0, 0)
+        turn_a(0, 1)
+        bases_scale_rows(1, 0)
+        bases_quant(0, 1)
+        product_b(0)
+        bases_turn(1, 0)
+        bases_scale_rows(1, 1)
+        bases_turn(1, 1)
+        bases_quant(1, 0)
+
+        for s in range(8):
+            turn_b(s)
+            if s == 2:
+                x_turn(1)
+            if s < 7:
+                spread(s + 1)
+                turn_a(s + 1, 0)
+            product_a(s, 0)
+            if s == 0:
+                bases_quant(1, 1)
+            else:
+                quant(s - 1, 1)
+            if s < 7:
+                turn_a(s + 1, 1)
+            product_a(s, 1)
+            if s == 3:
+                weights_quant(0)
+            quant(s, 0)
+            if s == 3:
+                weights_quant(1)
+            if s == 5:
+                y_out(0)
+            if s < 7:
+                product_b(s + 1)
+            gather_b(s)
+            if s == 2:
+                for g2 in range(4):
+                    weights_turn(g2)
+            if s < 6:
+                step1(s + 2)
+            if s == 3:
+                multiply(0)
+                multiply(1)
+            if s == 5:
+                y_quant(0)
+            if s >= 3:
+                multiply(s - 1)
+            if s == 6:
+                step3(0)
+                store(0, 0)
+                store(0, 1)
+        quant(7, 1)
+        multiply(7)
+        y_out(1)
+        y_quant(1)
+        step3(1)
+        store(1, 0)
+        store(1, 1)

@@ -12,10 +12,73 @@ U8 = mybir.dt.uint8
 FP8 = mybir.dt.float8_e4m3fn
 FP8X4 = mybir.dt.float8_e4m3fn_x4
 MULT = mybir.AluOpType.mult
+ADD = mybir.AluOpType.add
 COPY = mybir.ActivationFunctionType.Copy
 
 P = 128
-NB = (2, 3, 2, 3, 3, 3, 3, 3)
+GROUPS = 8
+HALF = GROUPS // 2
+J = 32
+
+GPSIMD_GROUPS = (0, 1, 1, 2, 1, 2, 1, 1)
+SCALAR_GROUPS = (3, 2, 2, 2, 2, 2, 2, 2)
+REPEATED_BY_SCALAR = (0,)
+
+TURN_RING = ("turn", 3)
+WORD_RING = ("word", 2)
+SIDE_RING = ("side", 1)
+X_HAT_RING = ("x_hat", 1)
+Y_RING = ("y", 1)
+
+ORDER = (
+    ("scale_turn",), ("scale_copy",), ("x_turn", 0), ("bases_scale_rows", 0, 0, 0), ("bases_scale_rows", 0, 0, 1),
+    ("d_spread", 1), ("bases_scale_rows", 0, 0, 3), ("bases_turn", 0, 0, 0), ("d_spread", 0), ("x_copy", 0),
+    ("bases_scale_rows", 0, 0, 2), ("bases_copy", 0, 0, 0), ("bases_scale_rows", 0, 1, 0),
+    ("bases_scale_rows", 0, 1, 2), ("d_spread_copy", 1), ("bases_turn", 0, 0, 1), ("bases_scale_rows", 0, 1, 1),
+    ("bases_copy", 0, 0, 1), ("d_spread_copy", 0), ("x_hat_matmul", 0), ("d_turn",), ("x_hat_matmul", 3),
+    ("x_hat_copy", 0), ("d_turned_copy",), ("repeat", 0), ("x_turn", 1), ("bases_scale_rows", 1, 0, 1),
+    ("x_hat_copy", 3), ("z_scalar", 0, 2), ("repeat_turn", 0, 1), ("repeat_turn", 0, 0), ("x_hat_matmul", 1),
+    ("bases_scale_rows", 1, 0, 0), ("bases_scale_rows", 0, 1, 3), ("bases_scale_rows", 1, 0, 2), ("repeat", 3),
+    ("z_scalar", 0, 0), ("x_hat_copy", 1), ("bases_scale_rows", 1, 0, 3), ("bases_quantize", 0, 0),
+    ("repeat_turn", 3, 0), ("x_hat_matmul", 2), ("z_scalar", 3, 1), ("z_scalar_turn", 0, 2), ("x_hat_copy", 2),
+    ("repeat_turn", 3, 1), ("z_vector", 0, 1), ("repeat", 1), ("repeat", 2), ("z_vector", 0, 0), ("x_copy", 1),
+    ("z_vector", 3, 0), ("gpsimd_copy", 3), ("repeat_turn", 1, 0), ("z_vector", 1, 0), ("bases_turn", 0, 1, 0),
+    ("z_scalar", 0, 1), ("x_hat_wide_matmul", 0), ("repeat_turn", 2, 1), ("bases_copy", 0, 1, 0),
+    ("bases_turn", 0, 1, 1), ("z_scalar", 3, 0), ("bases_scale_rows", 1, 1, 2), ("bases_copy", 0, 1, 1),
+    ("x_hat_wide_matmul", 1), ("x_hat_wide_matmul", 2), ("z_scalar", 2, 0), ("x_hat_wide_matmul", 3),
+    ("x_hat_wide_copy", 0), ("x_hat_wide_copy", 1), ("bases_scale_rows", 1, 1, 1), ("gpsimd_copy", 2),
+    ("z_gpsimd", 3, 1), ("repeat_turn", 2, 0), ("bases_scale_rows", 1, 1, 3), ("bases_turn", 1, 0, 0),
+    ("bases_copy", 1, 0, 0), ("bases_scale_rows", 1, 1, 0), ("z_quantize", 1, 0), ("z_gpsimd", 3, 0),
+    ("z_scalar_copy", 0, 2), ("repeat_turn", 1, 1), ("x_hat_turn", 0), ("z_quantize", 3, 0), ("x_hat_turn", 1),
+    ("gpsimd_copy", 1), ("x_hat_turned_copy", 1), ("x_hat_turned_copy", 0), ("z_scalar_turn", 0, 0), ("repeat", 5),
+    ("bases_turn", 1, 0, 1), ("bases_quantize", 0, 1), ("z_scalar_turn", 3, 0), ("z_vector", 2, 1),
+    ("bases_turn", 1, 1, 0), ("repeat", 6), ("bases_copy", 1, 0, 1), ("repeat", 4), ("z_vector", 1, 1),
+    ("z_gpsimd", 2, 0), ("z_vector", 2, 0), ("z_scalar", 2, 1), ("z_scalar", 1, 0), ("bases_copy", 1, 1, 0),
+    ("repeat_turn", 5, 0), ("bases_turn", 1, 1, 1), ("z_scalar_copy", 0, 0), ("repeat_turn", 5, 1),
+    ("z_scalar_turn", 2, 0), ("weights_turn", 0), ("z_vector", 5, 0), ("repeat", 7), ("z_scalar", 1, 1),
+    ("repeat_turn", 6, 1), ("bases_copy", 1, 1, 1), ("z_scalar_copy", 3, 0), ("gpsimd_copy", 5),
+    ("repeat_turn", 4, 0), ("weights_turn", 1), ("z_gpsimd", 5, 1), ("z_quantize", 0, 1), ("repeat_turn", 6, 0),
+    ("z_gpsimd", 1, 0), ("weights_turn", 2), ("z_scalar_copy", 2, 0), ("z_quantize", 3, 1), ("z_quantize", 2, 0),
+    ("weights_copy", 0), ("z_quantize", 0, 0), ("gpsimd_copy", 6), ("z_vector", 4, 0), ("z_scalar", 4, 0),
+    ("z_vector", 6, 1), ("weights_copy", 1), ("z_scalar_turn", 1, 0), ("repeat_turn", 7, 1), ("repeat_turn", 4, 1),
+    ("z_scalar", 7, 1), ("z_scalar", 4, 1), ("weights_turn", 3), ("weights_copy", 2), ("z_vector", 6, 0),
+    ("z_vector", 4, 1), ("z_scalar", 5, 1), ("z_quantize", 4, 0), ("repeat_turn", 7, 0), ("z_scalar_copy", 1, 0),
+    ("z_gpsimd", 5, 0), ("z_quantize", 2, 1), ("weights_copy", 3), ("weights_quantize", 0), ("z_gpsimd", 6, 0),
+    ("z_scalar_turn", 4, 0), ("gpsimd_copy", 7), ("z_scalar", 5, 0), ("gpsimd_copy", 4), ("z_gpsimd", 4, 0),
+    ("y_hat_matmul", 0, 0), ("weights_quantize", 1), ("z_scalar_copy", 4, 0), ("y_hat_matmul", 0, 1),
+    ("z_quantize", 6, 0), ("z_scalar", 7, 0), ("z_quantize", 1, 1), ("z_scalar_turn", 5, 0), ("y_hat_matmul", 1, 0),
+    ("y_hat_matmul", 1, 1), ("z_vector", 7, 1), ("z_scalar", 6, 1), ("y_hat_matmul", 2, 0), ("z_scalar", 6, 0),
+    ("z_vector", 7, 0), ("y_hat_matmul", 2, 1), ("y_hat_matmul", 3, 0), ("y_hat_matmul", 3, 1),
+    ("z_scalar_copy", 5, 0), ("z_scalar_turn", 7, 0), ("z_quantize", 5, 0), ("z_quantize", 4, 1), ("y_hat_copy", 0),
+    ("z_scalar_turn", 6, 0), ("y_hat_matmul", 4, 0), ("y_hat_quantize", 0), ("y_matmul", 0, 0), ("z_quantize", 5, 1),
+    ("z_scalar_copy", 6, 0), ("z_quantize", 6, 1), ("z_gpsimd", 7, 0), ("y_store", 0, 0), ("y_hat_matmul", 4, 1),
+    ("y_hat_matmul", 5, 0), ("z_scalar_copy", 7, 0), ("y_hat_matmul", 5, 1), ("z_quantize", 7, 0),
+    ("z_quantize", 7, 1), ("bases_quantize", 1, 0), ("y_matmul", 0, 1), ("y_hat_matmul", 6, 0),
+    ("y_hat_matmul", 6, 1), ("y_hat_matmul", 7, 0), ("y_matmul", 0, 2), ("y_hat_matmul", 7, 1),
+    ("bases_quantize", 1, 1), ("y_store", 0, 1), ("y_store", 0, 2), ("y_matmul", 0, 3), ("y_hat_copy", 1),
+    ("y_hat_quantize", 1), ("y_matmul", 1, 1), ("y_store", 0, 3), ("y_store", 1, 1), ("y_matmul", 1, 0),
+    ("y_matmul", 1, 2), ("y_matmul", 1, 3), ("y_store", 1, 2), ("y_store", 1, 3), ("y_store", 1, 0),
+)
 
 
 def tile_phydgalerkinconv_kernel(tc, x, wbases, bases_bytes, bases_scale, weights, D, out):
@@ -25,55 +88,66 @@ def tile_phydgalerkinconv_kernel(tc, x, wbases, bases_bytes, bases_scale, weight
         work = ctx.enter_context(tc.tile_pool(name="work", bufs=2))
         psum = ctx.enter_context(tc.psum_pool(name="psum", bufs=1))
 
-        sc4 = keep.tile([P, 4], F32, name="sc4")
-        nc.sync.dma_start(out=sc4[:], in_=bases_scale.rearrange("a b (p c) -> p (a b c)", c=4))
-        dpad = keep.tile([P, 512], BF16, name="dpad")
-        nc.vector.memset(dpad[:], 0.0)
-        nc.sync.dma_start(out=dpad[0:32, :], in_=D)
+        scale_col = keep.tile([P, 4], F32, name="scale_col")
+        d_rows = keep.tile([P, 512], BF16, name="d_rows")
         bytes_sb = [keep.tile([P, 2, 4, 512], U8, name="bytes0"), keep.tile([P, 2, 4, 512], U8, name="bytes1")]
         x_sb = [keep.tile([P, 1024], BF16, name="x0"), keep.tile([P, 1024], BF16, name="x1")]
         wb_sb = [keep.tile([P, 8, 512], BF16, name="wb0"), keep.tile([P, 8, 512], BF16, name="wb1")]
-        w_raw = keep.tile([P, P, 32], BF16, name="w_raw")
+        w_rows = keep.tile([P, P, J], BF16, name="w_rows")
 
         def load_bytes(b, h):
             nc.sync.dma_start(
-                out=bytes_sb[b][:, h], in_=bases_bytes[b].rearrange("(h p c) k -> h p c k", h=2, c=4)[h]
+                out=bytes_sb[b][:, h].rearrange("p (d e) k -> p d e k", d=2),
+                in_=bases_bytes[b].rearrange("(h d p e) k -> h p d e k", h=2, d=2, e=2)[h],
             )
 
-        def load_wb(b):
-            for q in range(2):
-                nc.sync.dma_start(
-                    out=wb_sb[b][:, 4 * q : 4 * q + 4, :],
-                    in_=wbases[b].rearrange("(c p) k -> p c k", p=P)[:, 4 * q : 4 * q + 4, :],
-                )
-
-        load_bytes(0, 0)
-        nc.sync.dma_start(out=x_sb[0][:], in_=x[0])
-        load_bytes(0, 1)
-        load_wb(0)
-        load_bytes(1, 0)
-        load_bytes(1, 1)
-        for q in range(2):
+        def load_wbases(b, half):
+            chunk = slice(4 * half, 4 * half + 4)
             nc.sync.dma_start(
-                out=w_raw[:, 64 * q : 64 * q + 64, :],
-                in_=weights.rearrange("i o j -> o i j")[:, 64 * q : 64 * q + 64, :],
+                out=wb_sb[b][:, chunk, :], in_=wbases[b].rearrange("(p c) k -> p c k", c=8)[:, chunk, :]
             )
+
+        def load_weights(half):
+            chunk = slice(64 * half, 64 * half + 64)
+            nc.sync.dma_start(out=w_rows[:, chunk, :], in_=weights.rearrange("i o j -> o i j")[:, chunk, :])
+
+        nc.sync.dma_start(out=scale_col[:], in_=bases_scale.rearrange("a b (p c) -> p (a b c)", c=4))
+        nc.vector.memset(d_rows[:], 0.0)
+        nc.sync.dma_start(out=x_sb[0][:], in_=x[0])
+        load_bytes(0, 0)
+        nc.sync.dma_start(out=d_rows[0:J, :], in_=D)
+        load_wbases(0, 0)
+        load_bytes(0, 1)
+        load_wbases(0, 1)
+        load_bytes(1, 0)
         nc.sync.dma_start(out=x_sb[1][:], in_=x[1])
-        load_wb(1)
+        load_bytes(1, 1)
+        load_wbases(1, 0)
+        load_wbases(1, 1)
+        load_weights(0)
+        load_weights(1)
 
         ident_f = keep.tile([P, P], F32, name="ident_f")
         make_identity(nc, ident_f[:])
         ident_b = keep.tile([P, P], BF16, name="ident_b")
-        sel = keep.tile([P, 4, P], BF16, name="sel")
+        select = keep.tile([P, 4, P], BF16, name="select")
         scale_rep = keep.tile([P, 512], F32, name="scale_rep")
-        drep = keep.tile([P, 4, P, 4], BF16, name="drep")
-        dt = keep.tile([P, 4, 32], BF16, name="dt")
+        d_rep = keep.tile([P, 4, P, 4], BF16, name="d_rep")
+        d_turned = keep.tile([P, 4, 2, 8, 2], BF16, name="d_turned")
         xt = [keep.tile([P, 8, P], BF16, name="xt0"), keep.tile([P, 8, P], BF16, name="xt1")]
-        bc = [keep.tile([P, 1024], U32, name="bc0", align_bytes=64), keep.tile([P, 1024], U32, name="bc1", align_bytes=64)]
-        bs = [keep.tile([P, 1024], U8, name="bs0", align_bytes=64), keep.tile([P, 1024], U8, name="bs1", align_bytes=64)]
-        wg = keep.tile([P, 4096], BF16, name="wg", align_bytes=64)
-        wc = keep.tile([P, 8, P], U32, name="wc", align_bytes=64)
-        ws = keep.tile([P, 8, P], U8, name="ws", align_bytes=64)
+        x_hat_wide = keep.tile([P, 4, P], F32, name="x_hat_wide")
+        x_hat = [keep.tile([P, 4, P], F32, name="x_hat0"), keep.tile([P, 4, P], F32, name="x_hat1")]
+        bases_codes = [
+            keep.tile([P, 1024], U32, name="bases_codes0", align_bytes=64),
+            keep.tile([P, 1024], U32, name="bases_codes1", align_bytes=64),
+        ]
+        bases_scales = [
+            keep.tile([P, 1024], U8, name="bases_scales0", align_bytes=64),
+            keep.tile([P, 1024], U8, name="bases_scales1", align_bytes=64),
+        ]
+        w_grouped = keep.tile([P, GROUPS * P * 4], BF16, name="w_grouped", align_bytes=64)
+        w_codes = keep.tile([P, GROUPS, P], U32, name="w_codes", align_bytes=64)
+        w_scales = keep.tile([P, GROUPS, P], U8, name="w_scales", align_bytes=64)
         warm = keep.tile([P, 1], F32, name="warm")
 
         ctx.enter_context(tc.manual_schedule())
@@ -81,292 +155,297 @@ def tile_phydgalerkinconv_kernel(tc, x, wbases, bases_bytes, bases_scale, weight
         nc.vector.memset(warm[:], 0.0)
         nc.scalar.activation(out=warm[:], in_=warm[:], func=COPY, scale=1.0)
         nc.vector.tensor_copy(out=ident_b[:], in_=ident_f[:])
-        for t in range(4):
+        for s in range(4):
             nc.vector.tensor_copy(
-                out=sel[:, t, :].rearrange("p (i q) -> p i q", q=8),
-                in_=ident_b[:, t:32:4].unsqueeze(1).to_broadcast([P, 16, 8]),
+                out=select[:, s, :].rearrange("p (c q) -> p c q", q=8),
+                in_=ident_b[:, s:J:4].unsqueeze(1).to_broadcast([P, 16, 8]),
             )
 
-        sc_ps = psum.tile([P, 4, P], F32, name="sc_ps", tag="A", bufs=3)
-        for c in range(4):
-            nc.tensor.transpose(sc_ps[:, c, :], sc4[:, c : c + 1].to_broadcast([P, P]), ident_f[:])
-        nc.vector.tensor_copy(
-            out=scale_rep[:].rearrange("p (n c) -> p n c", c=4), in_=sc_ps[:].rearrange("p c n -> p n c")
-        )
+        banks = {}
+        tiles = {}
 
-        dt_ps = psum.tile([P, 4, P], BF16, name="dt_ps", tag="W", bufs=2)
-        for t in range(4):
-            nc.tensor.transpose(dt_ps[:, t, :], dpad[:, t::4], ident_b[:])
-        nc.scalar.copy(out=dt[:], in_=dt_ps[:, :, 0:32])
-        d_perm = dpad[:].rearrange("p (m t) -> p t m", t=4)
-        for h in range(2):
-            d_ps = psum.tile([P, 4, 2, P], BF16, name="d_ps", tag="A", bufs=3)
-            for tj in range(4):
-                nc.tensor.matmul(
-                    d_ps[:, tj], lhsT=sel[:, tj, :], rhs=d_perm[:, 2 * h : 2 * h + 2, :], start=True, stop=True
-                )
-            (nc.vector.tensor_copy if h == 0 else nc.scalar.copy)(
-                out=drep[:, 2 * h : 2 * h + 2], in_=d_ps[:].rearrange("p j t m -> p t m j")
-            )
+        def new_bank(key, shape, ring, dtype=F32):
+            tag, count = ring
+            banks[key] = psum.tile(shape, dtype, name=key[0] + "_ps", tag=tag, bufs=count)
+            return banks[key]
 
-        bb = {}
-        bg = {}
+        def ring_tile(key, shape, dtype, count=2):
+            if key not in tiles:
+                tiles[key] = work.tile(shape, dtype, name=key[0], bufs=count, align_bytes=64)
+            return tiles[key]
 
-        def bases_scale_rows(b, h):
-            bb[b, h] = work.tile([P, 4, 512], BF16, name="bb")
+        def scale_turn():
+            bank = new_bank(("scale",), [P, 4, P], TURN_RING)
             for c in range(4):
-                nc.vector.tensor_tensor(
-                    out=bb[b, h][:, c, :], in0=bytes_sb[b][:, h, c, :].bitcast(FP8), in1=scale_rep[:], op=MULT
-                )
+                nc.tensor.transpose(bank[:, c, :], scale_col[:, c : c + 1].to_broadcast([P, P]), ident_f[:])
 
-        def bases_turn(b, h):
-            words = bb[b, h][:].rearrange("p c k -> p (c k)").bitcast(F32)
-            bg[b, h] = work.tile([P, 2048], BF16, name="bg", align_bytes=64)
-            dst = bg[b, h][:].bitcast(F32).rearrange("p (c n u) -> p c n u", c=4, u=2)
-            for c2 in range(2):
-                ps = psum.tile([P, 2, 2, P], F32, name="b_ps", tag="W", bufs=2)
-                for cc in range(2):
-                    c = 2 * c2 + cc
-                    for u in range(2):
-                        nc.tensor.transpose(ps[:, cc, u, :], words[:, 256 * c + u : 256 * (c + 1) : 2], ident_f[:])
-                nc.scalar.copy(out=dst[:, 2 * c2 : 2 * c2 + 2], in_=ps[:].rearrange("p c u n -> p c n u"))
-
-        def bases_quant(b, h):
-            cols = slice(512 * h, 512 * h + 512)
-            nc.vector.quantize_mx(out=bc[b][:, cols].bitcast(FP8X4), scales=bs[b][:, cols], in_=bg[b, h][:])
-
-        def x_turn(b):
-            ps = psum.tile([P, 8, P], BF16, name="x_ps", tag="W", bufs=2)
-            for c in range(8):
-                nc.tensor.transpose(ps[:, c, :], x_sb[b][:, P * c : P * (c + 1)], ident_b[:])
-            nc.scalar.copy(out=xt[b][:], in_=ps[:])
-
-        xh = {}
-        rep = {}
-        xsc = {}
-        xr = {}
-        zb = {}
-        wt = {}
-        z = {}
-        zc = {}
-        zs = {}
-        y_ps = {}
-
-        def step1(u):
-            b, t = divmod(u, 4)
-            xh[u] = psum.tile([P, P], F32, name="xh", tag="X", bufs=2)
-            for c in range(8):
-                nc.tensor.matmul(
-                    xh[u][:], lhsT=wb_sb[b][:, c, t::4], rhs=xt[b][:, c, :], start=(c == 0), stop=(c == 7)
-                )
-
-        def spread(u):
-            na = 16 * (8 - NB[u])
-            rep[u] = work.tile([P, P, 8], F32, name="rep")
-            nc.scalar.copy(
-                out=rep[u][:, :na, :], in_=xh[u][:, :na].unsqueeze(2).to_broadcast([P, na, 8])
-            )
-            xsc[u] = work.tile([P, 64], F32, name="xsc")
-            nc.scalar.copy(out=xsc[u][:, : P - na], in_=xh[u][:, na:])
-
-        def turn_a(u, part):
-            lo, hi = (0, 4) if part == 0 else (4, 8 - NB[u])
-            if hi == lo:
-                return
-            xr[u, part] = psum.tile([P, hi - lo, P], F32, name="xr", tag="A", bufs=3)
-            flat = rep[u][:].rearrange("p i r -> p (i r)")
-            for g in range(lo, hi):
-                nc.tensor.transpose(xr[u, part][:, g - lo, :], flat[:, P * g : P * (g + 1)], ident_f[:])
-
-        def product_a(u, part):
-            t = u % 4
-            lo, hi = (0, 4) if part == 0 else (4, 8 - NB[u])
-            if part == 0:
-                z[u] = work.tile([P, 8, P, 4], BF16, name="z", bufs=3, align_bytes=64)
-            if hi == lo:
-                return
-            shape = [P, hi - lo, P, 4]
-            nc.vector.tensor_tensor(
-                out=z[u][:, lo:hi],
-                in0=xr[u, part][:].unsqueeze(3).to_broadcast(shape),
-                in1=drep[:, t].unsqueeze(1).to_broadcast(shape),
-                op=MULT,
+        def scale_copy():
+            nc.vector.tensor_copy(
+                out=scale_rep[:].rearrange("p (n c) -> p n c", c=4),
+                in_=banks["scale",][:].rearrange("p c n -> p n c"),
             )
 
-        def product_b(u):
-            t = u % 4
-            zb[u] = work.tile([P, 4 * 512], BF16, name="zb")
-            for i in range(16 * NB[u]):
-                nc.scalar.activation(
-                    out=zb[u][:, 32 * i : 32 * i + 32], in_=dt[:, t, :], func=COPY, scale=xsc[u][:, i : i + 1]
-                )
+        def d_turn():
+            bank = new_bank(("d_turned",), [P, 4, P], WORD_RING, BF16)
+            for t in range(4):
+                nc.tensor.transpose(bank[:, t, :], d_rows[:, t::4], ident_b[:])
 
-        def turn_b(u):
-            words = zb[u][:].bitcast(F32)
-            for g0 in range(0, NB[u], 2):
-                n = min(2, NB[u] - g0)
-                wt[u, g0] = psum.tile([P, n, 2, P], F32, name="wt", tag="W", bufs=2)
-                for g in range(n):
-                    base = 256 * (g0 + g)
-                    for w in range(2):
-                        nc.tensor.transpose(wt[u, g0][:, g, w, :], words[:, base + w : base + 256 : 2], ident_f[:])
-
-        def gather_b(u):
-            na = 8 - NB[u]
-            dst = z[u][:].rearrange("p g k t -> p (g k t)").bitcast(F32).rearrange("p (g k w) -> p g k w", g=8, w=2)
-            for g0 in range(0, NB[u], 2):
-                n = min(2, NB[u] - g0)
+        def d_turned_copy():
+            for t in range(4):
                 nc.scalar.copy(
-                    out=dst[:, na + g0 : na + g0 + n], in_=wt[u, g0][:].rearrange("p g w k -> p g k w")
+                    out=d_turned[:, t],
+                    in_=banks["d_turned",][:, t, 0:J].rearrange("p (q v e) -> p v q e", v=2, e=2),
                 )
 
-        def quant(u, half):
-            if half == 0:
-                zc[u] = work.tile([P, 8, P], U32, name="zc", bufs=8, align_bytes=64)
-                zs[u] = work.tile([P, 8, P], U8, name="zs", bufs=8, align_bytes=64)
-            gs = slice(4 * half, 4 * half + 4)
-            nc.vector.quantize_mx(
-                out=zc[u][:, gs, :].rearrange("p g k -> p (g k)").bitcast(FP8X4),
-                scales=zs[u][:, gs, :].rearrange("p g k -> p (g k)"),
-                in_=z[u][:, gs].rearrange("p g k t -> p (g k t)"),
-            )
-
-        def multiply(u):
-            b, t = divmod(u, 4)
-            if t == 0:
-                y_ps[b] = psum.tile([P, 4, P], F32, name="y_ps", tag="Y", bufs=1)
-            for g in range(8):
-                nc.tensor.matmul_mx(
-                    out=y_ps[b][:, t, :],
-                    lhsT=zc[u][:, g, :].bitcast(FP8X4),
-                    lhsT_scale=zs[u][:, g, :],
-                    rhs=wc[:, g, :].bitcast(FP8X4),
-                    rhs_scale=ws[:, g, :],
-                    start=(g == 0),
-                    stop=(g == 7),
-                )
-
-        def weights_turn(g2):
-            words = w_raw[:].rearrange("p i j -> p (i j)").bitcast(F32)
-            dst = wg[:].bitcast(F32).rearrange("p (g n w) -> p g n w", g=8, w=2)
-            ps = psum.tile([P, 2, 2, P], F32, name="w_ps", tag="W", bufs=2)
-            for g in range(2):
-                base = 256 * (2 * g2 + g)
-                for w in range(2):
-                    nc.tensor.transpose(ps[:, g, w, :], words[:, base + w : base + 256 : 2], ident_f[:])
-            nc.scalar.copy(out=dst[:, 2 * g2 : 2 * g2 + 2], in_=ps[:].rearrange("p g w n -> p g n w"))
-
-        def weights_quant(half):
-            gs = slice(4 * half, 4 * half + 4)
-            nc.vector.quantize_mx(
-                out=wc[:, gs, :].rearrange("p g n -> p (g n)").bitcast(FP8X4),
-                scales=ws[:, gs, :].rearrange("p g n -> p (g n)"),
-                in_=wg[:, 2048 * half : 2048 * half + 2048],
-            )
-
-        yc = {}
-        ys = {}
-        yb = {}
-        o_ps = {}
-        o_sb = {}
-
-        def y_out(b):
-            yb[b] = work.tile([P, P, 4], BF16, name="yb", align_bytes=64)
-            nc.scalar.copy(out=yb[b][:], in_=y_ps[b][:].rearrange("p t o -> p o t"))
-
-        def y_quant(b):
-            yc[b] = work.tile([P, P], U32, name="yc", align_bytes=64)
-            ys[b] = work.tile([P, P], U8, name="ys", align_bytes=64)
-            nc.vector.quantize_mx(
-                out=yc[b][:].bitcast(FP8X4), scales=ys[b][:], in_=yb[b][:].rearrange("p o t -> p (o t)")
-            )
-
-        def step3(b):
-            for h in range(2):
-                o_ps[b, h] = psum.tile([P, 512], F32, name="o_ps", tag="W", bufs=2)
-                cols = slice(512 * h, 512 * h + 512)
-                nc.tensor.matmul_mx(
-                    out=o_ps[b, h][:],
-                    lhsT=yc[b][:].bitcast(FP8X4),
-                    lhsT_scale=ys[b][:],
-                    rhs=bc[b][:, cols].bitcast(FP8X4),
-                    rhs_scale=bs[b][:, cols],
+        def d_spread(half):
+            bank = new_bank(("d_spread", half), [P, 4, 2, P], TURN_RING, BF16)
+            for s in range(4):
+                nc.tensor.matmul(
+                    bank[:, s],
+                    lhsT=select[:, s, :],
+                    rhs=d_rows[:].rearrange("p (m t) -> p t m", t=4)[:, 2 * half : 2 * half + 2, :],
                     start=True,
                     stop=True,
                 )
 
-        def store(b, h):
-            o_sb[b, h] = work.tile([P, 512], F32, name="o_sb")
-            (nc.vector.tensor_copy if b == 1 and h == 0 else nc.scalar.copy)(
-                out=o_sb[b, h][:].rearrange("o (p c) -> o p c", c=4),
-                in_=o_ps[b, h][:].rearrange("o (c p) -> o p c", c=4),
+        def d_spread_copy(half):
+            nc.scalar.copy(
+                out=d_rep[:, 2 * half : 2 * half + 2],
+                in_=banks["d_spread", half][:].rearrange("p s t m -> p t m s"),
             )
-            nc.sync.dma_start(out=out[b][:, 512 * h : 512 * h + 512], in_=o_sb[b, h][:])
 
-        bases_scale_rows(0, 0)
-        bases_turn(0, 0)
-        x_turn(0)
-        bases_scale_rows(0, 1)
-        bases_turn(0, 1)
-        bases_quant(0, 0)
-        step1(0)
-        spread(0)
-        step1(1)
-        turn_a(0, 0)
-        turn_a(0, 1)
-        bases_scale_rows(1, 0)
-        bases_quant(0, 1)
-        product_b(0)
-        bases_turn(1, 0)
-        bases_scale_rows(1, 1)
-        bases_turn(1, 1)
-        bases_quant(1, 0)
+        def bases_scale_rows(b, h, r):
+            rows = ring_tile(("bases_rows", b, h), [P, 4, 512], BF16)
+            nc.vector.tensor_tensor(
+                out=rows[:, r, :], in0=bytes_sb[b][:, h, r, :].bitcast(FP8), in1=scale_rep[:], op=MULT
+            )
 
-        for s in range(8):
-            turn_b(s)
-            if s == 2:
-                x_turn(1)
-            if s < 7:
-                spread(s + 1)
-                turn_a(s + 1, 0)
-            product_a(s, 0)
-            if s == 0:
-                bases_quant(1, 1)
+        def bases_turn(b, h, pair):
+            words = tiles["bases_rows", b, h][:].rearrange("p r k -> p (r k)").bitcast(F32)
+            bank = new_bank(("bases", b, h, pair), [P, 2, 2, P], SIDE_RING)
+            for a in range(2):
+                r = 2 * pair + a
+                for v in range(2):
+                    nc.tensor.transpose(bank[:, v, a, :], words[:, 256 * r + v : 256 * (r + 1) : 2], ident_f[:])
+
+        def bases_copy(b, h, pair):
+            grouped = ring_tile(("bases_grouped", b, h), [P, 2048], BF16)
+            words = grouped[:].bitcast(F32).rearrange("p (r n v) -> p r n v", r=4, v=2)
+            nc.scalar.copy(
+                out=words[:, 2 * pair : 2 * pair + 2], in_=banks["bases", b, h, pair][:].rearrange("p v a n -> p a n v")
+            )
+
+        def bases_quantize(b, h):
+            cols = slice(512 * h, 512 * h + 512)
+            nc.vector.quantize_mx(
+                out=bases_codes[b][:, cols].bitcast(FP8X4),
+                scales=bases_scales[b][:, cols],
+                in_=tiles["bases_grouped", b, h][:],
+            )
+
+        def weights_turn(pair):
+            words = w_rows[:].rearrange("p i j -> p (i j)").bitcast(F32)
+            bank = new_bank(("weights", pair), [P, 2, 2, P], SIDE_RING)
+            for a in range(2):
+                first = 256 * (2 * pair + a)
+                for v in range(2):
+                    nc.tensor.transpose(bank[:, a, v, :], words[:, first + v : first + 256 : 2], ident_f[:])
+
+        def weights_copy(pair):
+            words = w_grouped[:].bitcast(F32).rearrange("p (g o v) -> p g o v", g=GROUPS, v=2)
+            nc.scalar.copy(
+                out=words[:, 2 * pair : 2 * pair + 2], in_=banks["weights", pair][:].rearrange("p a v o -> p a o v")
+            )
+
+        def weights_quantize(half):
+            groups = slice(HALF * half, HALF * half + HALF)
+            nc.vector.quantize_mx(
+                out=w_codes[:, groups, :].rearrange("p g o -> p (g o)").bitcast(FP8X4),
+                scales=w_scales[:, groups, :].rearrange("p g o -> p (g o)"),
+                in_=w_grouped[:, 2048 * half : 2048 * half + 2048],
+            )
+
+        def x_turn(b):
+            bank = new_bank(("x", b), [P, 8, P], SIDE_RING, BF16)
+            for c in range(8):
+                nc.tensor.transpose(bank[:, c, :], x_sb[b][:, c::8], ident_b[:])
+
+        def x_copy(b):
+            nc.scalar.copy(out=xt[b][:], in_=banks["x", b][:])
+
+        def x_hat_matmul(t):
+            bank = new_bank(("x_hat", t), [P, P], WORD_RING if t % 2 else X_HAT_RING)
+            for c in range(8):
+                nc.tensor.matmul(bank[:], lhsT=wb_sb[0][:, c, t::4], rhs=xt[0][:, c, :], start=(c == 0), stop=(c == 7))
+
+        def x_hat_copy(t):
+            nc.scalar.copy(out=x_hat[0][:, t, :], in_=banks["x_hat", t][:])
+
+        def x_hat_wide_matmul(pair):
+            bank = new_bank(("x_hat_wide",), [P, 512], X_HAT_RING) if pair == 0 else banks["x_hat_wide",]
+            for c in range(2 * pair, 2 * pair + 2):
+                nc.tensor.matmul(bank[:], lhsT=xt[1][:, c, :], rhs=wb_sb[1][:, c, :], start=(c == 0), stop=(c == 7))
+
+        def x_hat_wide_copy(part):
+            ts = slice(0, 1) if part == 0 else slice(1, 4)
+            nc.scalar.copy(
+                out=x_hat_wide[:, ts, :], in_=banks["x_hat_wide",][:].rearrange("i (m t) -> i t m", t=4)[:, ts, :]
+            )
+
+        def x_hat_turn(part):
+            bank = new_bank(("x_hat_turned",), [P, 4, P], X_HAT_RING) if part == 0 else banks["x_hat_turned",]
+            for t in range(1) if part == 0 else range(1, 4):
+                nc.tensor.transpose(bank[:, t, :], x_hat_wide[:, t, :], ident_f[:])
+
+        def x_hat_turned_copy(part):
+            ts = slice(0, 1) if part == 0 else slice(1, 4)
+            nc.scalar.copy(out=x_hat[1][:, ts, :], in_=banks["x_hat_turned",][:, ts, :])
+
+        def repeat(u):
+            b, t = divmod(u, 4)
+            channels = 16 * (GROUPS - SCALAR_GROUPS[u])
+            repeated = ring_tile(("repeated", u), [P, P, 8], F32, 4)
+            source = x_hat[b][:, t, :channels].unsqueeze(2).to_broadcast([P, channels, 8])
+            if u in REPEATED_BY_SCALAR:
+                nc.scalar.copy(out=repeated[:, :channels, :], in_=source)
             else:
-                quant(s - 1, 1)
-            if s < 7:
-                turn_a(s + 1, 1)
-            product_a(s, 1)
-            if s == 3:
-                weights_quant(0)
-            quant(s, 0)
-            if s == 3:
-                weights_quant(1)
-            if s == 5:
-                y_out(0)
-            if s < 7:
-                product_b(s + 1)
-            gather_b(s)
-            if s == 2:
-                for g2 in range(4):
-                    weights_turn(g2)
-            if s < 6:
-                step1(s + 2)
-            if s == 3:
-                multiply(0)
-                multiply(1)
-            if s == 5:
-                y_quant(0)
-            if s >= 3:
-                multiply(s - 1)
-            if s == 6:
-                step3(0)
-                store(0, 0)
-                store(0, 1)
-        quant(7, 1)
-        multiply(7)
-        y_out(1)
-        y_quant(1)
-        step3(1)
-        store(1, 0)
-        store(1, 1)
+                nc.gpsimd.tensor_scalar(
+                    out=repeated[:, :channels, :], in0=source, scalar1=1.0, scalar2=0.0, op0=MULT, op1=ADD
+                )
+
+        def repeat_turn(u, half):
+            first, end = (0, HALF) if half == 0 else (HALF, GROUPS - SCALAR_GROUPS[u])
+            bank = new_bank(("repeated", u, half), [P, end - first, P], TURN_RING)
+            columns = tiles["repeated", u][:].rearrange("p i q -> p (i q)")
+            for g in range(first, end):
+                nc.tensor.transpose(bank[:, g - first, :], columns[:, P * g : P * (g + 1)], ident_f[:])
+
+        def z_tile(u):
+            return ring_tile(("z", u), [P, GROUPS, P, 4], BF16, 6)
+
+        def z_vector(u, half):
+            first, end = (0, HALF) if half == 0 else (HALF + GPSIMD_GROUPS[u], GROUPS - SCALAR_GROUPS[u])
+            turned = banks["repeated", u, half][:, first - HALF * half : end - HALF * half]
+            shape = [P, end - first, P, 4]
+            nc.vector.tensor_tensor(
+                out=z_tile(u)[:, first:end],
+                in0=turned.unsqueeze(3).to_broadcast(shape),
+                in1=d_rep[:, u % 4].unsqueeze(1).to_broadcast(shape),
+                op=MULT,
+            )
+
+        def gpsimd_copy(u):
+            count = GPSIMD_GROUPS[u]
+            turned = ring_tile(("turned", u), [P, 2, P], F32, 3)
+            nc.scalar.copy(out=turned[:, :count, :], in_=banks["repeated", u, 1][:, :count, :])
+
+        def z_gpsimd(u, a):
+            nc.gpsimd.tensor_tensor(
+                out=z_tile(u)[:, HALF + a],
+                in0=tiles["turned", u][:, a, :].unsqueeze(2).to_broadcast([P, P, 4]),
+                in1=d_rep[:, u % 4],
+                op=MULT,
+            )
+
+        def z_scalar(u, a):
+            b, t = divmod(u, 4)
+            products = ring_tile(("products", u), [P, 4, 2, 16, 16], BF16, 3)
+            for c in range(16):
+                i = 16 * (GROUPS - SCALAR_GROUPS[u] + a) + c
+                nc.scalar.activation(
+                    out=products[:, a, :, c, :],
+                    in_=d_turned[:, t].rearrange("p v q e -> p v (q e)"),
+                    func=COPY,
+                    scale=x_hat[b][:, t, i : i + 1],
+                )
+
+        def z_scalar_turn(u, first):
+            count = min(2, SCALAR_GROUPS[u] - first)
+            bank = new_bank(("products", u, first), [P, count, 2, P], WORD_RING)
+            words = tiles["products", u][:].rearrange("p a v c k -> p (a v c k)").bitcast(F32)
+            for a in range(count):
+                for v in range(2):
+                    start = 256 * (first + a) + 128 * v
+                    nc.tensor.transpose(bank[:, a, v, :], words[:, start : start + 128], ident_f[:])
+
+        def z_scalar_copy(u, first):
+            count = min(2, SCALAR_GROUPS[u] - first)
+            words = z_tile(u)[:].rearrange("p g m s -> p (g m s)").bitcast(F32).rearrange("p (g m v) -> p g m v", g=GROUPS, v=2)
+            g = GROUPS - SCALAR_GROUPS[u] + first
+            nc.scalar.copy(
+                out=words[:, g : g + count], in_=banks["products", u, first][:].rearrange("p a v m -> p a m v")
+            )
+
+        def z_quantize(u, half):
+            codes = ring_tile(("z_codes", u), [P, GROUPS, P], U32, 8)
+            scales = ring_tile(("z_scales", u), [P, GROUPS, P], U8, 8)
+            groups = slice(HALF * half, HALF * half + HALF)
+            nc.vector.quantize_mx(
+                out=codes[:, groups, :].rearrange("p g m -> p (g m)").bitcast(FP8X4),
+                scales=scales[:, groups, :].rearrange("p g m -> p (g m)"),
+                in_=tiles["z", u][:, groups].rearrange("p g m s -> p (g m s)"),
+            )
+
+        def y_hat_matmul(u, half):
+            b, t = divmod(u, 4)
+            bank = new_bank(("y_hat", b), [P, 4, P], Y_RING) if t == 0 and half == 0 else banks["y_hat", b]
+            for g in range(HALF * half, HALF * half + HALF):
+                nc.tensor.matmul_mx(
+                    out=bank[:, t, :],
+                    lhsT=tiles["z_codes", u][:, g, :].bitcast(FP8X4),
+                    lhsT_scale=tiles["z_scales", u][:, g, :],
+                    rhs=w_codes[:, g, :].bitcast(FP8X4),
+                    rhs_scale=w_scales[:, g, :],
+                    start=(g == 0),
+                    stop=(g == GROUPS - 1),
+                )
+
+        def y_hat_copy(b):
+            grouped = ring_tile(("y_hat_grouped", b), [P, P, 4], BF16)
+            nc.scalar.copy(out=grouped[:], in_=banks["y_hat", b][:].rearrange("p t o -> p o t"))
+
+        def y_hat_quantize(b):
+            codes = ring_tile(("y_hat_codes", b), [P, P], U32)
+            scales = ring_tile(("y_hat_scales", b), [P, P], U8)
+            nc.vector.quantize_mx(
+                out=codes[:].bitcast(FP8X4),
+                scales=scales[:],
+                in_=tiles["y_hat_grouped", b][:].rearrange("p o t -> p (o t)"),
+            )
+
+        def y_matmul(b, quarter):
+            bank = new_bank(("y", b, quarter), [P, 256], TURN_RING if b == 1 and quarter < 3 else SIDE_RING)
+            cols = slice(256 * quarter, 256 * quarter + 256)
+            nc.tensor.matmul_mx(
+                out=bank[:],
+                lhsT=tiles["y_hat_codes", b][:].bitcast(FP8X4),
+                lhsT_scale=tiles["y_hat_scales", b][:],
+                rhs=bases_codes[b][:, cols].bitcast(FP8X4),
+                rhs_scale=bases_scales[b][:, cols],
+                start=True,
+                stop=True,
+            )
+
+        def y_store(b, quarter):
+            y = ring_tile(("y", b, quarter), [P, 256], F32, 8)
+            (nc.vector.tensor_copy if b == 1 and quarter % 2 == 0 else nc.scalar.copy)(
+                out=y[:].rearrange("o (p e) -> o p e", e=2),
+                in_=banks["y", b, quarter][:].rearrange("o (e p) -> o p e", e=2),
+            )
+            nc.sync.dma_start(out=out[b][:, 256 * quarter : 256 * quarter + 256], in_=y[:])
+
+        tasks = {
+            "scale_turn": scale_turn, "scale_copy": scale_copy, "d_turn": d_turn, "d_turned_copy": d_turned_copy,
+            "d_spread": d_spread, "d_spread_copy": d_spread_copy, "bases_scale_rows": bases_scale_rows,
+            "bases_turn": bases_turn, "bases_copy": bases_copy, "bases_quantize": bases_quantize,
+            "weights_turn": weights_turn, "weights_copy": weights_copy, "weights_quantize": weights_quantize,
+            "x_turn": x_turn, "x_copy": x_copy, "x_hat_matmul": x_hat_matmul, "x_hat_copy": x_hat_copy,
+            "x_hat_wide_matmul": x_hat_wide_matmul, "x_hat_wide_copy": x_hat_wide_copy, "x_hat_turn": x_hat_turn,
+            "x_hat_turned_copy": x_hat_turned_copy, "repeat": repeat, "repeat_turn": repeat_turn,
+            "gpsimd_copy": gpsimd_copy, "z_gpsimd": z_gpsimd, "z_vector": z_vector, "z_scalar": z_scalar,
+            "z_scalar_turn": z_scalar_turn, "z_scalar_copy": z_scalar_copy, "z_quantize": z_quantize,
+            "y_hat_matmul": y_hat_matmul, "y_hat_copy": y_hat_copy, "y_hat_quantize": y_hat_quantize,
+            "y_matmul": y_matmul, "y_store": y_store,
+        }
+        for task, *arguments in ORDER:
+            tasks[task](*arguments)

from contextlib import ExitStack

import concourse.mybir as mybir
from concourse.masks import make_identity

FLOPS = 1610612736

F32 = mybir.dt.float32
BF16 = mybir.dt.bfloat16
U32 = mybir.dt.uint32
U8 = mybir.dt.uint8
FP8 = mybir.dt.float8_e4m3fn
FP8X4 = mybir.dt.float8_e4m3fn_x4
MULT = mybir.AluOpType.mult
ADD = mybir.AluOpType.add
COPY = mybir.ActivationFunctionType.Copy

P = 128
GROUPS = 8
HALF = GROUPS // 2
J = 32

GPSIMD_GROUPS = (0, 1, 1, 2, 1, 2, 1, 1)
SCALAR_GROUPS = (3, 2, 2, 2, 2, 2, 2, 2)
REPEATED_BY_SCALAR = (0,)

TURN_RING = ("turn", 3)
WORD_RING = ("word", 2)
SIDE_RING = ("side", 1)
X_HAT_RING = ("x_hat", 1)
Y_RING = ("y", 1)

ORDER = (
    ("scale_turn",), ("scale_copy",), ("x_turn", 0), ("bases_scale_rows", 0, 0, 0), ("bases_scale_rows", 0, 0, 1),
    ("d_spread", 1), ("bases_scale_rows", 0, 0, 3), ("bases_turn", 0, 0, 0), ("d_spread", 0), ("x_copy", 0),
    ("bases_scale_rows", 0, 0, 2), ("bases_copy", 0, 0, 0), ("bases_scale_rows", 0, 1, 0),
    ("bases_scale_rows", 0, 1, 2), ("d_spread_copy", 1), ("bases_turn", 0, 0, 1), ("bases_scale_rows", 0, 1, 1),
    ("bases_copy", 0, 0, 1), ("d_spread_copy", 0), ("x_hat_matmul", 0), ("d_turn",), ("x_hat_matmul", 3),
    ("x_hat_copy", 0), ("d_turned_copy",), ("repeat", 0), ("x_turn", 1), ("bases_scale_rows", 1, 0, 1),
    ("x_hat_copy", 3), ("z_scalar", 0, 2), ("repeat_turn", 0, 1), ("repeat_turn", 0, 0), ("x_hat_matmul", 1),
    ("bases_scale_rows", 1, 0, 0), ("bases_scale_rows", 0, 1, 3), ("bases_scale_rows", 1, 0, 2), ("repeat", 3),
    ("z_scalar", 0, 0), ("x_hat_copy", 1), ("bases_scale_rows", 1, 0, 3), ("bases_quantize", 0, 0),
    ("repeat_turn", 3, 0), ("x_hat_matmul", 2), ("z_scalar", 3, 1), ("z_scalar_turn", 0, 2), ("x_hat_copy", 2),
    ("repeat_turn", 3, 1), ("z_vector", 0, 1), ("repeat", 1), ("repeat", 2), ("z_vector", 0, 0), ("x_copy", 1),
    ("z_vector", 3, 0), ("gpsimd_copy", 3), ("repeat_turn", 1, 0), ("z_vector", 1, 0), ("bases_turn", 0, 1, 0),
    ("z_scalar", 0, 1), ("x_hat_wide_matmul", 0), ("repeat_turn", 2, 1), ("bases_copy", 0, 1, 0),
    ("bases_turn", 0, 1, 1), ("z_scalar", 3, 0), ("bases_scale_rows", 1, 1, 2), ("bases_copy", 0, 1, 1),
    ("x_hat_wide_matmul", 1), ("x_hat_wide_matmul", 2), ("z_scalar", 2, 0), ("x_hat_wide_matmul", 3),
    ("x_hat_wide_copy", 0), ("x_hat_wide_copy", 1), ("bases_scale_rows", 1, 1, 1), ("gpsimd_copy", 2),
    ("z_gpsimd", 3, 1), ("repeat_turn", 2, 0), ("bases_scale_rows", 1, 1, 3), ("bases_turn", 1, 0, 0),
    ("bases_copy", 1, 0, 0), ("bases_scale_rows", 1, 1, 0), ("z_quantize", 1, 0), ("z_gpsimd", 3, 0),
    ("z_scalar_copy", 0, 2), ("repeat_turn", 1, 1), ("x_hat_turn", 0), ("z_quantize", 3, 0), ("x_hat_turn", 1),
    ("gpsimd_copy", 1), ("x_hat_turned_copy", 1), ("x_hat_turned_copy", 0), ("z_scalar_turn", 0, 0), ("repeat", 5),
    ("bases_turn", 1, 0, 1), ("bases_quantize", 0, 1), ("z_scalar_turn", 3, 0), ("z_vector", 2, 1),
    ("bases_turn", 1, 1, 0), ("repeat", 6), ("bases_copy", 1, 0, 1), ("repeat", 4), ("z_vector", 1, 1),
    ("z_gpsimd", 2, 0), ("z_vector", 2, 0), ("z_scalar", 2, 1), ("z_scalar", 1, 0), ("bases_copy", 1, 1, 0),
    ("repeat_turn", 5, 0), ("bases_turn", 1, 1, 1), ("z_scalar_copy", 0, 0), ("repeat_turn", 5, 1),
    ("z_scalar_turn", 2, 0), ("weights_turn", 0), ("z_vector", 5, 0), ("repeat", 7), ("z_scalar", 1, 1),
    ("repeat_turn", 6, 1), ("bases_copy", 1, 1, 1), ("z_scalar_copy", 3, 0), ("gpsimd_copy", 5),
    ("repeat_turn", 4, 0), ("weights_turn", 1), ("z_gpsimd", 5, 1), ("z_quantize", 0, 1), ("repeat_turn", 6, 0),
    ("z_gpsimd", 1, 0), ("weights_turn", 2), ("z_scalar_copy", 2, 0), ("z_quantize", 3, 1), ("z_quantize", 2, 0),
    ("weights_copy", 0), ("z_quantize", 0, 0), ("gpsimd_copy", 6), ("z_vector", 4, 0), ("z_scalar", 4, 0),
    ("z_vector", 6, 1), ("weights_copy", 1), ("z_scalar_turn", 1, 0), ("repeat_turn", 7, 1), ("repeat_turn", 4, 1),
    ("z_scalar", 7, 1), ("z_scalar", 4, 1), ("weights_turn", 3), ("weights_copy", 2), ("z_vector", 6, 0),
    ("z_vector", 4, 1), ("z_scalar", 5, 1), ("z_quantize", 4, 0), ("repeat_turn", 7, 0), ("z_scalar_copy", 1, 0),
    ("z_gpsimd", 5, 0), ("z_quantize", 2, 1), ("weights_copy", 3), ("weights_quantize", 0), ("z_gpsimd", 6, 0),
    ("z_scalar_turn", 4, 0), ("gpsimd_copy", 7), ("z_scalar", 5, 0), ("gpsimd_copy", 4), ("z_gpsimd", 4, 0),
    ("y_hat_matmul", 0, 0), ("weights_quantize", 1), ("z_scalar_copy", 4, 0), ("y_hat_matmul", 0, 1),
    ("z_quantize", 6, 0), ("z_scalar", 7, 0), ("z_quantize", 1, 1), ("z_scalar_turn", 5, 0), ("y_hat_matmul", 1, 0),
    ("y_hat_matmul", 1, 1), ("z_vector", 7, 1), ("z_scalar", 6, 1), ("y_hat_matmul", 2, 0), ("z_scalar", 6, 0),
    ("z_vector", 7, 0), ("y_hat_matmul", 2, 1), ("y_hat_matmul", 3, 0), ("y_hat_matmul", 3, 1),
    ("z_scalar_copy", 5, 0), ("z_scalar_turn", 7, 0), ("z_quantize", 5, 0), ("z_quantize", 4, 1), ("y_hat_copy", 0),
    ("z_scalar_turn", 6, 0), ("y_hat_matmul", 4, 0), ("y_hat_quantize", 0), ("y_matmul", 0, 0), ("z_quantize", 5, 1),
    ("z_scalar_copy", 6, 0), ("z_quantize", 6, 1), ("z_gpsimd", 7, 0), ("y_store", 0, 0), ("y_hat_matmul", 4, 1),
    ("y_hat_matmul", 5, 0), ("z_scalar_copy", 7, 0), ("y_hat_matmul", 5, 1), ("z_quantize", 7, 0),
    ("z_quantize", 7, 1), ("bases_quantize", 1, 0), ("y_matmul", 0, 1), ("y_hat_matmul", 6, 0),
    ("y_hat_matmul", 6, 1), ("y_hat_matmul", 7, 0), ("y_matmul", 0, 2), ("y_hat_matmul", 7, 1),
    ("bases_quantize", 1, 1), ("y_store", 0, 1), ("y_store", 0, 2), ("y_matmul", 0, 3), ("y_hat_copy", 1),
    ("y_hat_quantize", 1), ("y_matmul", 1, 1), ("y_store", 0, 3), ("y_store", 1, 1), ("y_matmul", 1, 0),
    ("y_matmul", 1, 2), ("y_matmul", 1, 3), ("y_store", 1, 2), ("y_store", 1, 3), ("y_store", 1, 0),
)


def tile_phydgalerkinconv_kernel(tc, x, wbases, bases_bytes, bases_scale, weights, D, out):
    nc = tc.nc
    with ExitStack() as ctx:
        keep = ctx.enter_context(tc.tile_pool(name="keep", bufs=1))
        work = ctx.enter_context(tc.tile_pool(name="work", bufs=2))
        psum = ctx.enter_context(tc.psum_pool(name="psum", bufs=1))

        scale_col = keep.tile([P, 4], F32, name="scale_col")
        d_rows = keep.tile([P, 512], BF16, name="d_rows")
        bytes_sb = [keep.tile([P, 2, 4, 512], U8, name="bytes0"), keep.tile([P, 2, 4, 512], U8, name="bytes1")]
        x_sb = [keep.tile([P, 1024], BF16, name="x0"), keep.tile([P, 1024], BF16, name="x1")]
        wb_sb = [keep.tile([P, 8, 512], BF16, name="wb0"), keep.tile([P, 8, 512], BF16, name="wb1")]
        w_rows = keep.tile([P, P, J], BF16, name="w_rows")

        def load_bytes(b, h):
            nc.sync.dma_start(
                out=bytes_sb[b][:, h].rearrange("p (d e) k -> p d e k", d=2),
                in_=bases_bytes[b].rearrange("(h d p e) k -> h p d e k", h=2, d=2, e=2)[h],
            )

        def load_wbases(b, half):
            chunk = slice(4 * half, 4 * half + 4)
            nc.sync.dma_start(
                out=wb_sb[b][:, chunk, :], in_=wbases[b].rearrange("(p c) k -> p c k", c=8)[:, chunk, :]
            )

        def load_weights(half):
            chunk = slice(64 * half, 64 * half + 64)
            nc.sync.dma_start(out=w_rows[:, chunk, :], in_=weights.rearrange("i o j -> o i j")[:, chunk, :])

        nc.sync.dma_start(out=scale_col[:], in_=bases_scale.rearrange("a b (p c) -> p (a b c)", c=4))
        nc.vector.memset(d_rows[:], 0.0)
        nc.sync.dma_start(out=x_sb[0][:], in_=x[0])
        load_bytes(0, 0)
        nc.sync.dma_start(out=d_rows[0:J, :], in_=D)
        load_wbases(0, 0)
        load_bytes(0, 1)
        load_wbases(0, 1)
        load_bytes(1, 0)
        nc.sync.dma_start(out=x_sb[1][:], in_=x[1])
        load_bytes(1, 1)
        load_wbases(1, 0)
        load_wbases(1, 1)
        load_weights(0)
        load_weights(1)

        ident_f = keep.tile([P, P], F32, name="ident_f")
        make_identity(nc, ident_f[:])
        ident_b = keep.tile([P, P], BF16, name="ident_b")
        select = keep.tile([P, 4, P], BF16, name="select")
        scale_rep = keep.tile([P, 512], F32, name="scale_rep")
        d_rep = keep.tile([P, 4, P, 4], BF16, name="d_rep")
        d_turned = keep.tile([P, 4, 2, 8, 2], BF16, name="d_turned")
        xt = [keep.tile([P, 8, P], BF16, name="xt0"), keep.tile([P, 8, P], BF16, name="xt1")]
        x_hat_wide = keep.tile([P, 4, P], F32, name="x_hat_wide")
        x_hat = [keep.tile([P, 4, P], F32, name="x_hat0"), keep.tile([P, 4, P], F32, name="x_hat1")]
        bases_codes = [
            keep.tile([P, 1024], U32, name="bases_codes0", align_bytes=64),
            keep.tile([P, 1024], U32, name="bases_codes1", align_bytes=64),
        ]
        bases_scales = [
            keep.tile([P, 1024], U8, name="bases_scales0", align_bytes=64),
            keep.tile([P, 1024], U8, name="bases_scales1", align_bytes=64),
        ]
        w_grouped = keep.tile([P, GROUPS * P * 4], BF16, name="w_grouped", align_bytes=64)
        w_codes = keep.tile([P, GROUPS, P], U32, name="w_codes", align_bytes=64)
        w_scales = keep.tile([P, GROUPS, P], U8, name="w_scales", align_bytes=64)
        warm = keep.tile([P, 1], F32, name="warm")

        ctx.enter_context(tc.manual_schedule())

        nc.vector.memset(warm[:], 0.0)
        nc.scalar.activation(out=warm[:], in_=warm[:], func=COPY, scale=1.0)
        nc.vector.tensor_copy(out=ident_b[:], in_=ident_f[:])
        for s in range(4):
            nc.vector.tensor_copy(
                out=select[:, s, :].rearrange("p (c q) -> p c q", q=8),
                in_=ident_b[:, s:J:4].unsqueeze(1).to_broadcast([P, 16, 8]),
            )

        banks = {}
        tiles = {}

        def new_bank(key, shape, ring, dtype=F32):
            tag, count = ring
            banks[key] = psum.tile(shape, dtype, name=key[0] + "_ps", tag=tag, bufs=count)
            return banks[key]

        def ring_tile(key, shape, dtype, count=2):
            if key not in tiles:
                tiles[key] = work.tile(shape, dtype, name=key[0], bufs=count, align_bytes=64)
            return tiles[key]

        def scale_turn():
            bank = new_bank(("scale",), [P, 4, P], TURN_RING)
            for c in range(4):
                nc.tensor.transpose(bank[:, c, :], scale_col[:, c : c + 1].to_broadcast([P, P]), ident_f[:])

        def scale_copy():
            nc.vector.tensor_copy(
                out=scale_rep[:].rearrange("p (n c) -> p n c", c=4),
                in_=banks["scale",][:].rearrange("p c n -> p n c"),
            )

        def d_turn():
            bank = new_bank(("d_turned",), [P, 4, P], WORD_RING, BF16)
            for t in range(4):
                nc.tensor.transpose(bank[:, t, :], d_rows[:, t::4], ident_b[:])

        def d_turned_copy():
            for t in range(4):
                nc.scalar.copy(
                    out=d_turned[:, t],
                    in_=banks["d_turned",][:, t, 0:J].rearrange("p (q v e) -> p v q e", v=2, e=2),
                )

        def d_spread(half):
            bank = new_bank(("d_spread", half), [P, 4, 2, P], TURN_RING, BF16)
            for s in range(4):
                nc.tensor.matmul(
                    bank[:, s],
                    lhsT=select[:, s, :],
                    rhs=d_rows[:].rearrange("p (m t) -> p t m", t=4)[:, 2 * half : 2 * half + 2, :],
                    start=True,
                    stop=True,
                )

        def d_spread_copy(half):
            nc.scalar.copy(
                out=d_rep[:, 2 * half : 2 * half + 2],
                in_=banks["d_spread", half][:].rearrange("p s t m -> p t m s"),
            )

        def bases_scale_rows(b, h, r):
            rows = ring_tile(("bases_rows", b, h), [P, 4, 512], BF16)
            nc.vector.tensor_tensor(
                out=rows[:, r, :], in0=bytes_sb[b][:, h, r, :].bitcast(FP8), in1=scale_rep[:], op=MULT
            )

        def bases_turn(b, h, pair):
            words = tiles["bases_rows", b, h][:].rearrange("p r k -> p (r k)").bitcast(F32)
            bank = new_bank(("bases", b, h, pair), [P, 2, 2, P], SIDE_RING)
            for a in range(2):
                r = 2 * pair + a
                for v in range(2):
                    nc.tensor.transpose(bank[:, v, a, :], words[:, 256 * r + v : 256 * (r + 1) : 2], ident_f[:])

        def bases_copy(b, h, pair):
            grouped = ring_tile(("bases_grouped", b, h), [P, 2048], BF16)
            words = grouped[:].bitcast(F32).rearrange("p (r n v) -> p r n v", r=4, v=2)
            nc.scalar.copy(
                out=words[:, 2 * pair : 2 * pair + 2], in_=banks["bases", b, h, pair][:].rearrange("p v a n -> p a n v")
            )

        def bases_quantize(b, h):
            cols = slice(512 * h, 512 * h + 512)
            nc.vector.quantize_mx(
                out=bases_codes[b][:, cols].bitcast(FP8X4),
                scales=bases_scales[b][:, cols],
                in_=tiles["bases_grouped", b, h][:],
            )

        def weights_turn(pair):
            words = w_rows[:].rearrange("p i j -> p (i j)").bitcast(F32)
            bank = new_bank(("weights", pair), [P, 2, 2, P], SIDE_RING)
            for a in range(2):
                first = 256 * (2 * pair + a)
                for v in range(2):
                    nc.tensor.transpose(bank[:, a, v, :], words[:, first + v : first + 256 : 2], ident_f[:])

        def weights_copy(pair):
            words = w_grouped[:].bitcast(F32).rearrange("p (g o v) -> p g o v", g=GROUPS, v=2)
            nc.scalar.copy(
                out=words[:, 2 * pair : 2 * pair + 2], in_=banks["weights", pair][:].rearrange("p a v o -> p a o v")
            )

        def weights_quantize(half):
            groups = slice(HALF * half, HALF * half + HALF)
            nc.vector.quantize_mx(
                out=w_codes[:, groups, :].rearrange("p g o -> p (g o)").bitcast(FP8X4),
                scales=w_scales[:, groups, :].rearrange("p g o -> p (g o)"),
                in_=w_grouped[:, 2048 * half : 2048 * half + 2048],
            )

        def x_turn(b):
            bank = new_bank(("x", b), [P, 8, P], SIDE_RING, BF16)
            for c in range(8):
                nc.tensor.transpose(bank[:, c, :], x_sb[b][:, c::8], ident_b[:])

        def x_copy(b):
            nc.scalar.copy(out=xt[b][:], in_=banks["x", b][:])

        def x_hat_matmul(t):
            bank = new_bank(("x_hat", t), [P, P], WORD_RING if t % 2 else X_HAT_RING)
            for c in range(8):
                nc.tensor.matmul(bank[:], lhsT=wb_sb[0][:, c, t::4], rhs=xt[0][:, c, :], start=(c == 0), stop=(c == 7))

        def x_hat_copy(t):
            nc.scalar.copy(out=x_hat[0][:, t, :], in_=banks["x_hat", t][:])

        def x_hat_wide_matmul(pair):
            bank = new_bank(("x_hat_wide",), [P, 512], X_HAT_RING) if pair == 0 else banks["x_hat_wide",]
            for c in range(2 * pair, 2 * pair + 2):
                nc.tensor.matmul(bank[:], lhsT=xt[1][:, c, :], rhs=wb_sb[1][:, c, :], start=(c == 0), stop=(c == 7))

        def x_hat_wide_copy(part):
            ts = slice(0, 1) if part == 0 else slice(1, 4)
            nc.scalar.copy(
                out=x_hat_wide[:, ts, :], in_=banks["x_hat_wide",][:].rearrange("i (m t) -> i t m", t=4)[:, ts, :]
            )

        def x_hat_turn(part):
            bank = new_bank(("x_hat_turned",), [P, 4, P], X_HAT_RING) if part == 0 else banks["x_hat_turned",]
            for t in range(1) if part == 0 else range(1, 4):
                nc.tensor.transpose(bank[:, t, :], x_hat_wide[:, t, :], ident_f[:])

        def x_hat_turned_copy(part):
            ts = slice(0, 1) if part == 0 else slice(1, 4)
            nc.scalar.copy(out=x_hat[1][:, ts, :], in_=banks["x_hat_turned",][:, ts, :])

        def repeat(u):
            b, t = divmod(u, 4)
            channels = 16 * (GROUPS - SCALAR_GROUPS[u])
            repeated = ring_tile(("repeated", u), [P, P, 8], F32, 4)
            source = x_hat[b][:, t, :channels].unsqueeze(2).to_broadcast([P, channels, 8])
            if u in REPEATED_BY_SCALAR:
                nc.scalar.copy(out=repeated[:, :channels, :], in_=source)
            else:
                nc.gpsimd.tensor_scalar(
                    out=repeated[:, :channels, :], in0=source, scalar1=1.0, scalar2=0.0, op0=MULT, op1=ADD
                )

        def repeat_turn(u, half):
            first, end = (0, HALF) if half == 0 else (HALF, GROUPS - SCALAR_GROUPS[u])
            bank = new_bank(("repeated", u, half), [P, end - first, P], TURN_RING)
            columns = tiles["repeated", u][:].rearrange("p i q -> p (i q)")
            for g in range(first, end):
                nc.tensor.transpose(bank[:, g - first, :], columns[:, P * g : P * (g + 1)], ident_f[:])

        def z_tile(u):
            return ring_tile(("z", u), [P, GROUPS, P, 4], BF16, 6)

        def z_vector(u, half):
            first, end = (0, HALF) if half == 0 else (HALF + GPSIMD_GROUPS[u], GROUPS - SCALAR_GROUPS[u])
            turned = banks["repeated", u, half][:, first - HALF * half : end - HALF * half]
            shape = [P, end - first, P, 4]
            nc.vector.tensor_tensor(
                out=z_tile(u)[:, first:end],
                in0=turned.unsqueeze(3).to_broadcast(shape),
                in1=d_rep[:, u % 4].unsqueeze(1).to_broadcast(shape),
                op=MULT,
            )

        def gpsimd_copy(u):
            count = GPSIMD_GROUPS[u]
            turned = ring_tile(("turned", u), [P, 2, P], F32, 3)
            nc.scalar.copy(out=turned[:, :count, :], in_=banks["repeated", u, 1][:, :count, :])

        def z_gpsimd(u, a):
            nc.gpsimd.tensor_tensor(
                out=z_tile(u)[:, HALF + a],
                in0=tiles["turned", u][:, a, :].unsqueeze(2).to_broadcast([P, P, 4]),
                in1=d_rep[:, u % 4],
                op=MULT,
            )

        def z_scalar(u, a):
            b, t = divmod(u, 4)
            products = ring_tile(("products", u), [P, 4, 2, 16, 16], BF16, 3)
            for c in range(16):
                i = 16 * (GROUPS - SCALAR_GROUPS[u] + a) + c
                nc.scalar.activation(
                    out=products[:, a, :, c, :],
                    in_=d_turned[:, t].rearrange("p v q e -> p v (q e)"),
                    func=COPY,
                    scale=x_hat[b][:, t, i : i + 1],
                )

        def z_scalar_turn(u, first):
            count = min(2, SCALAR_GROUPS[u] - first)
            bank = new_bank(("products", u, first), [P, count, 2, P], WORD_RING)
            words = tiles["products", u][:].rearrange("p a v c k -> p (a v c k)").bitcast(F32)
            for a in range(count):
                for v in range(2):
                    start = 256 * (first + a) + 128 * v
                    nc.tensor.transpose(bank[:, a, v, :], words[:, start : start + 128], ident_f[:])

        def z_scalar_copy(u, first):
            count = min(2, SCALAR_GROUPS[u] - first)
            words = z_tile(u)[:].rearrange("p g m s -> p (g m s)").bitcast(F32).rearrange("p (g m v) -> p g m v", g=GROUPS, v=2)
            g = GROUPS - SCALAR_GROUPS[u] + first
            nc.scalar.copy(
                out=words[:, g : g + count], in_=banks["products", u, first][:].rearrange("p a v m -> p a m v")
            )

        def z_quantize(u, half):
            codes = ring_tile(("z_codes", u), [P, GROUPS, P], U32, 8)
            scales = ring_tile(("z_scales", u), [P, GROUPS, P], U8, 8)
            groups = slice(HALF * half, HALF * half + HALF)
            nc.vector.quantize_mx(
                out=codes[:, groups, :].rearrange("p g m -> p (g m)").bitcast(FP8X4),
                scales=scales[:, groups, :].rearrange("p g m -> p (g m)"),
                in_=tiles["z", u][:, groups].rearrange("p g m s -> p (g m s)"),
            )

        def y_hat_matmul(u, half):
            b, t = divmod(u, 4)
            bank = new_bank(("y_hat", b), [P, 4, P], Y_RING) if t == 0 and half == 0 else banks["y_hat", b]
            for g in range(HALF * half, HALF * half + HALF):
                nc.tensor.matmul_mx(
                    out=bank[:, t, :],
                    lhsT=tiles["z_codes", u][:, g, :].bitcast(FP8X4),
                    lhsT_scale=tiles["z_scales", u][:, g, :],
                    rhs=w_codes[:, g, :].bitcast(FP8X4),
                    rhs_scale=w_scales[:, g, :],
                    start=(g == 0),
                    stop=(g == GROUPS - 1),
                )

        def y_hat_copy(b):
            grouped = ring_tile(("y_hat_grouped", b), [P, P, 4], BF16)
            nc.scalar.copy(out=grouped[:], in_=banks["y_hat", b][:].rearrange("p t o -> p o t"))

        def y_hat_quantize(b):
            codes = ring_tile(("y_hat_codes", b), [P, P], U32)
            scales = ring_tile(("y_hat_scales", b), [P, P], U8)
            nc.vector.quantize_mx(
                out=codes[:].bitcast(FP8X4),
                scales=scales[:],
                in_=tiles["y_hat_grouped", b][:].rearrange("p o t -> p (o t)"),
            )

        def y_matmul(b, quarter):
            bank = new_bank(("y", b, quarter), [P, 256], TURN_RING if b == 1 and quarter < 3 else SIDE_RING)
            cols = slice(256 * quarter, 256 * quarter + 256)
            nc.tensor.matmul_mx(
                out=bank[:],
                lhsT=tiles["y_hat_codes", b][:].bitcast(FP8X4),
                lhsT_scale=tiles["y_hat_scales", b][:],
                rhs=bases_codes[b][:, cols].bitcast(FP8X4),
                rhs_scale=bases_scales[b][:, cols],
                start=True,
                stop=True,
            )

        def y_store(b, quarter):
            y = ring_tile(("y", b, quarter), [P, 256], F32, 8)
            (nc.vector.tensor_copy if b == 1 and quarter % 2 == 0 else nc.scalar.copy)(
                out=y[:].rearrange("o (p e) -> o p e", e=2),
                in_=banks["y", b, quarter][:].rearrange("o (e p) -> o p e", e=2),
            )
            nc.sync.dma_start(out=out[b][:, 256 * quarter : 256 * quarter + 256], in_=y[:])

        tasks = {
            "scale_turn": scale_turn, "scale_copy": scale_copy, "d_turn": d_turn, "d_turned_copy": d_turned_copy,
            "d_spread": d_spread, "d_spread_copy": d_spread_copy, "bases_scale_rows": bases_scale_rows,
            "bases_turn": bases_turn, "bases_copy": bases_copy, "bases_quantize": bases_quantize,
            "weights_turn": weights_turn, "weights_copy": weights_copy, "weights_quantize": weights_quantize,
            "x_turn": x_turn, "x_copy": x_copy, "x_hat_matmul": x_hat_matmul, "x_hat_copy": x_hat_copy,
            "x_hat_wide_matmul": x_hat_wide_matmul, "x_hat_wide_copy": x_hat_wide_copy, "x_hat_turn": x_hat_turn,
            "x_hat_turned_copy": x_hat_turned_copy, "repeat": repeat, "repeat_turn": repeat_turn,
            "gpsimd_copy": gpsimd_copy, "z_gpsimd": z_gpsimd, "z_vector": z_vector, "z_scalar": z_scalar,
            "z_scalar_turn": z_scalar_turn, "z_scalar_copy": z_scalar_copy, "z_quantize": z_quantize,
            "y_hat_matmul": y_hat_matmul, "y_hat_copy": y_hat_copy, "y_hat_quantize": y_hat_quantize,
            "y_matmul": y_matmul, "y_store": y_store,
        }
        for task, *arguments in ORDER:
            tasks[task](*arguments)
